import numpy as np
import ml_dtypes


def mxq(x, axis, fmt="e4m3"):
    dtype, down = {"e4m3": (ml_dtypes.float8_e4m3fn, 7), "e5m2": (ml_dtypes.float8_e5m2, 14)}[fmt]
    v = np.moveaxis(np.asarray(x, np.float32).astype(ml_dtypes.bfloat16).astype(np.float64), axis, -1)
    blocks = v.reshape(v.shape[:-1] + (-1, 32))
    amax = np.abs(blocks).max(-1, keepdims=True)
    byte = np.maximum(np.where(amax > 0, np.frexp(amax)[1] - 1 + 127, 0) - down, 1)
    scale = np.exp2(byte - 127.0)
    codes = (blocks / scale).astype(np.float32).astype(dtype).astype(np.float64)
    return np.moveaxis((codes * scale).reshape(v.shape), -1, axis)


WIDE = False


def mx_kscale(k):
    if not WIDE:
        return np.ones(k)
    levels = np.array([18, -18])
    if k % 512:
        return np.exp2(np.random.permutation(np.resize(levels, k // 32))).repeat(32)
    a = np.empty((k // 512, 16))
    for p in range(k // 512):
        a[p, :8] = np.random.permutation(np.resize(levels, 8))
        for g in range(8):
            far = levels[np.abs(levels - a[p, g]) >= 10]
            a[p, g + 8] = far[np.random.randint(len(far))]
    return np.exp2(a.ravel()).repeat(32)


BF16 = ml_dtypes.bfloat16


def bf(x):
    return np.asarray(x, np.float32).astype(BF16)


def f64(x):
    return np.asarray(x).astype(np.float64)


B, IN, HID, N, NM = 2, 512, 512, 512, 5
C = IN + HID
K = NM * C


def setup_inputs():
    s = mx_kscale(C)
    fj = mx_kscale(HID)
    fn = mx_kscale(N)
    top = np.max(fn)
    x0 = bf(np.random.standard_normal((B, C, N)) * 0.8)
    xa0 = bf(np.random.standard_normal((B, C, N)) * 0.55)
    xb0 = bf(np.random.standard_normal((B, C, N)) * 0.55)
    s0 = bf(np.random.standard_normal((N, N)) * 0.7 / np.sqrt(N))
    s1 = bf(np.random.standard_normal((N, N)) * 0.7 / np.sqrt(N))
    w0 = bf(np.random.standard_normal((K, HID)) / np.sqrt(K))
    b_c = bf(0.3 * np.random.standard_normal(HID))
    u = bf(1.0 / (1.0 + np.exp(-(1.0 + np.random.standard_normal((B, HID, N))))))
    hx = bf(np.random.standard_normal((B, HID, N)))
    g = bf(8.0 * np.random.standard_normal((B, HID, N)) * np.exp2(np.random.randint(-6, 1, (B, 1, N))) * fj[None, :, None] * fn[None, None, :] / top)
    x2a = 2.0 * (f64(xa0) @ f64(s0).T) - f64(x0)
    x2b = 2.0 * (f64(xb0) @ f64(s1).T) - f64(x0)
    h = np.concatenate([f64(x0), f64(xa0), x2a, f64(xb0), x2b], axis=1)
    cand = np.tanh(f64(w0).T @ h + f64(b_c)[None, :, None])
    return {"x_cand": x0,
            "x1_0": bf(f64(xa0) * s[None, :, None]),
            "x1_1": xb0,
            "support0": bf(f64(s0) / fn[:, None] * fn[None, :]),
            "support1": s1,
            "W_c": bf(f64(w0) / np.tile(s, NM)[:, None] / fj[None, :]),
            "b_c": b_c,
            "u": u,
            "hx": hx,
            "cand": np.asarray(cand, np.float32),
            "grad_out": g}


def reference(x_cand, x1_0, x1_1, support0, support1, W_c, b_c, u, hx, cand, grad_out):
    cf = f64(cand)
    dz2 = f64(grad_out) * (1.0 - f64(u)) * (1.0 - cf * cf)
    wsel = f64(W_c)[C:3 * C]
    dh = mxq(wsel, 1, "e4m3") @ mxq(dz2, 1, "e5m2")
    dz1 = (2.0 * dh[:, C:]).reshape(B * C, N)
    dx = mxq(dz1, 1, "e5m2") @ mxq(f64(support0), 0, "e4m3")
    dx = dx.reshape(B, C, N) + dh[:, :C]
    ds = mxq(dz1, 0, "e5m2").T @ mxq(f64(x1_0).reshape(B * C, N), 0, "e4m3")
    return dx, ds

@@ -1,0 +1,345 @@
+from contextlib import ExitStack
+
+import concourse.mybir as mybir
+from concourse.masks import make_identity
+
+B, HID, N, C = 2, 512, 512, 1024
+FLOPS = 2 * B * 2 * C * HID * N + 2 * B * C * N * N + 2 * B * C * N * N
+BYTES = 2 * (2 * B * HID * N + 2 * C * HID + N * N + B * C * N) + 4 * (B * HID * N + B * C * N + N * N)
+
+F32 = mybir.dt.float32
+BF16 = mybir.dt.bfloat16
+U32 = mybir.dt.uint32
+U8 = mybir.dt.uint8
+E4M3 = mybir.dt.float8_e4m3fn_x4
+E5M2 = mybir.dt.float8_e5m2_x4
+ALU = mybir.AluOpType
+ACT = mybir.ActivationFunctionType
+
+P = 128
+PACK = 4
+K = P * PACK
+WIDE = PACK * 512
+
+
+def tile_dcgrucell_pc_v_kernel(
+    tc, x_cand, x1_0, x1_1, support0, support1, W_c, b_c, u, hx, cand, grad_out, out_0, out_1
+):
+    nc = tc.nc
+    with ExitStack() as ctx:
+        keep = ctx.enter_context(tc.tile_pool(name="keep", bufs=1))
+        work = ctx.enter_context(tc.tile_pool(name="work", bufs=2))
+        psum = ctx.enter_context(tc.psum_pool(name="psum", bufs=1))
+        ctx.enter_context(tc.manual_schedule())
+
+        def load(name, rows, dtype, half=None):
+            view = rows.rearrange("(p j) w -> p j w", j=PACK)
+            if half is not None:
+                view = view[:, 2 * half : 2 * half + 2, :]
+            width = view.shape[1] * view.shape[2]
+            raw = keep.tile([P, width], dtype, name=name, align_bytes=64)
+            nc.sync.dma_start(out=raw[:], in_=view.rearrange("p j w -> p (j w)"))
+            return raw
+
+        def load_gates(b):
+            tiles = []
+            for h in range(2):
+                tiles.append(
+                    (
+                        load("u%d%d" % (b, h), u[b], BF16, h),
+                        load("g%d%d" % (b, h), grad_out[b], BF16, h),
+                        load("c%d%d" % (b, h), cand[b], F32, h),
+                    )
+                )
+            return tiles
+
+        def load_w(block, g):
+            r0 = C * block + K * g
+            return load("w%d%d" % (block, g), W_c[r0 : r0 + K, :], BF16)
+
+        w_raw = {}
+        gates = [load_gates(0)]
+        w_raw[2, 0] = load_w(2, 0)
+        w_raw[2, 1] = load_w(2, 1)
+        sup_raw = load("sup", support0, BF16)
+        w_raw[1, 0] = load_w(1, 0)
+        gates.append(load_gates(1))
+        w_raw[1, 1] = load_w(1, 1)
+        units = [(b, g) for b in range(B) for g in range(C // K)]
+        x_raw = {}
+        for i in range(4):
+            x_raw[i] = load("x%d" % i, x1_0[units[i][0], K * units[i][1] : K * units[i][1] + K, :], BF16)
+
+        ident0 = keep.tile([P, P], F32, name="ident0")
+        make_identity(nc, ident0[:])
+        ident = keep.tile([P, P], F32, name="ident")
+        nc.scalar.activation(out=ident[:], in_=ident0[:], func=ACT.Square)
+
+        free_banks = list(range(8))
+        bank_of = {}
+
+        def take_bank():
+            n = free_banks[0]
+            free_banks.remove(n)
+            bank = psum.tile([P, 512], F32, name="bank%d" % n, tag="bank%d" % n)
+            bank_of[n] = bank
+            return bank
+
+        def give_bank(bank):
+            free_banks.extend([n for n in range(8) if bank_of.get(n) is bank])
+
+        def copy_on(eng, out, in_):
+            if eng == "s":
+                nc.scalar.copy(out=out, in_=in_)
+            else:
+                nc.vector.tensor_copy(out=out, in_=in_)
+
+        def quantize(name, grouped, fmt):
+            codes = keep.tile([P, 512], U32, name=name + "_codes", align_bytes=64)
+            scales = keep.tile([P, 512], U8, name=name + "_scales", align_bytes=64)
+            nc.vector.quantize_mx(out=codes[:].bitcast(fmt), scales=scales[:], in_=grouped[:])
+            return (codes, scales, fmt)
+
+        def mx(acc, stat, s, mov, start, stop):
+            cols = slice(P * s, P * (s + 1))
+            nc.tensor.matmul_mx(
+                out=acc[:],
+                lhsT=stat[0][:, cols].bitcast(stat[2]),
+                lhsT_scale=stat[1][:, cols],
+                rhs=mov[0][:].bitcast(mov[2]),
+                rhs_scale=mov[1][:],
+                start=start,
+                stop=stop,
+            )
+
+        def interleave(eng, raw):
+            grouped = work.tile([P, WIDE], BF16, name="grouped", tag="grouped", bufs=3, align_bytes=64)
+            copy_on(
+                eng,
+                grouped[:].rearrange("p (c i t) -> p c t i", i=4, t=PACK),
+                raw[:].rearrange("p (t c i) -> p c t i", i=4, t=PACK),
+            )
+            return grouped
+
+        def interleave_support(eng, raw):
+            grouped = work.tile([P, WIDE], BF16, name="grouped", tag="grouped", bufs=3, align_bytes=64)
+            copy_on(
+                eng,
+                grouped[:].rearrange("p (c i u e) -> p c u e i", i=4, u=2, e=2),
+                raw[:].rearrange("p (e u c i) -> p c u e i", i=4, u=2, e=2),
+            )
+            return grouped
+
+        def transposes(src, stepped):
+            words = src[:].bitcast(F32)
+            banks = []
+            for pair in range(2):
+                bank = take_bank()
+                for t2 in range(2):
+                    for h in range(2):
+                        w0 = 256 * (2 * pair + t2)
+                        if stepped:
+                            in_ = words[:, w0 + h : w0 + 256 : 2]
+                        else:
+                            in_ = words[:, w0 + P * h : w0 + P * (h + 1)]
+                        slot = 2 * t2 + h
+                        nc.tensor.transpose(bank[:, P * slot : P * (slot + 1)], in_, ident[:])
+                banks.append(bank)
+            return banks
+
+        def empty_transposes(engs, banks):
+            turned = work.tile([P, WIDE], BF16, name="turned", tag="turned", bufs=3, align_bytes=64)
+            words = turned[:].bitcast(F32)
+            for pair in range(2):
+                copy_on(
+                    engs[pair],
+                    words[:, 512 * pair : 512 * (pair + 1)].rearrange("p (t c h) -> p t c h", t=2, h=2),
+                    banks[pair][:].rearrange("p (t h c) -> p t c h", t=2, h=2),
+                )
+                give_bank(banks[pair])
+            return turned
+
+        def gate_product(b, h):
+            a = work.tile([P, 1024], F32, name="a", tag="a")
+            nc.vector.scalar_tensor_tensor(
+                out=a[:], in0=gates[b][h][0][:], scalar=1.0, in1=gates[b][h][1][:], op0=ALU.subtract, op1=ALU.mult
+            )
+            return a
+
+        def square(b, h):
+            s = work.tile([P, 1024], F32, name="s", tag="s")
+            nc.scalar.activation(
+                out=s[:].rearrange("p (n e) -> p n e", e=2),
+                in_=gates[b][h][2][:].rearrange("p (e n) -> p n e", e=2),
+                func=ACT.Square,
+            )
+            return s
+
+        def dz2_half(dz2, h, s, a):
+            nc.vector.scalar_tensor_tensor(
+                out=dz2[:, 1024 * h : 1024 * (h + 1)].rearrange("p (n e) -> p n e", e=2),
+                in0=s[:].rearrange("p (n e) -> p n e", e=2),
+                scalar=1.0,
+                in1=a[:].rearrange("p (e n) -> p n e", e=2),
+                op0=ALU.subtract,
+                op1=ALU.mult,
+            )
+
+        def interleave_pairs(dz2):
+            grouped = work.tile([P, WIDE], BF16, name="grouped", tag="grouped", bufs=3, align_bytes=64)
+            nc.vector.tensor_copy(
+                out=grouped[:].bitcast(F32).rearrange("p (n h) -> p n h", h=2),
+                in_=dz2[:].bitcast(F32).rearrange("p (h n) -> p n h", h=2),
+            )
+            return grouped
+
+        wq = {}
+        dz2q = {}
+        dz1 = {}
+        dz1_nodes = {}
+        dz1_chan = {}
+        xq = {}
+
+        def dh_x2(i, slots=range(PACK)):
+            b, g = units[i]
+            banks = []
+            for t in slots:
+                bank = take_bank()
+                mx(bank, wq[2, g], t, dz2q[b], True, True)
+                banks.append(bank)
+            return banks
+
+        def round_dz1(i, banks, engs):
+            dz1[i] = keep.tile([P, WIDE], BF16, name="dz1_%d" % i, align_bytes=64)
+            for t in range(PACK):
+                out = dz1[i][:, 512 * t : 512 * (t + 1)].rearrange("p (h q) -> p h q", h=2)
+                in_ = banks[t][:].rearrange("p (q h) -> p h q", h=2)
+                if engs[t] == "s":
+                    nc.scalar.activation(out=out, in_=in_, func=ACT.Copy, scale=2.0)
+                else:
+                    nc.vector.tensor_scalar(out=out, in0=in_, scalar1=2.0, scalar2=None, op0=ALU.mult)
+                give_bank(banks[t])
+
+        def dx_pair(i, pair):
+            b, g = units[i]
+            banks = []
+            for t in (2 * pair, 2 * pair + 1):
+                bank = take_bank()
+                mx(bank, wq[1, g], t, dz2q[b], True, False)
+                mx(bank, dz1_nodes[i], t, supq, False, True)
+                banks.append(bank)
+            return banks
+
+        def store_pair(banks, engs, dst, split=False):
+            res = work.tile([P, 1024], F32, name="res", tag="res", bufs=5)
+            for k in range(2):
+                copy_on(engs[k], res[:, 512 * k : 512 * (k + 1)], banks[k][:])
+                give_bank(banks[k])
+                if split:
+                    nc.sync.dma_start(out=dst[:, 512 * k : 512 * (k + 1)], in_=res[:, 512 * k : 512 * (k + 1)])
+            if not split:
+                nc.sync.dma_start(out=dst, in_=res[:])
+
+        def out0_view(i, pair):
+            b, g = units[i]
+            rows = out_0[b, K * g : K * (g + 1), :].rearrange("(p t) m -> p (t m)", t=PACK)
+            return rows[:, 1024 * pair : 1024 * (pair + 1)]
+
+        a0 = gate_product(0, 0)
+        s0 = square(0, 0)
+        a1 = gate_product(0, 1)
+        s1 = square(0, 1)
+        dz2 = work.tile([P, WIDE], BF16, name="dz2", tag="dz2")
+        dz2_half(dz2, 0, s0, a0)
+        dz2_half(dz2, 1, s1, a1)
+        tw = transposes(w_raw[2, 0], True)
+        turned = empty_transposes("ss", tw)
+        grouped = interleave_pairs(dz2)
+        tw = transposes(w_raw[2, 1], True)
+        dz2q[0] = quantize("dz20", grouped, E5M2)
+        wq[2, 0] = quantize("w20", turned, E4M3)
+        m0 = dh_x2(0)
+        turned = empty_transposes("ss", tw)
+        sup_g = interleave_support("v", sup_raw)
+        a0 = gate_product(1, 0)
+        wq[2, 1] = quantize("w21", turned, E4M3)
+        supq = quantize("sup", sup_g, E4M3)
+        tw = transposes(w_raw[1, 0], True)
+        round_dz1(0, m0, "ssss")
+        ta = transposes(dz1[0], False)
+        a1 = gate_product(1, 1)
+        s0 = square(1, 0)
+        s1 = square(1, 1)
+        m1 = dh_x2(1)
+        dz2 = work.tile([P, WIDE], BF16, name="dz2", tag="dz2")
+        dz2_half(dz2, 0, s0, a0)
+        dz2_half(dz2, 1, s1, a1)
+        turned_a = empty_transposes("ss", ta)
+        tw2 = transposes(w_raw[1, 1], True)
+        turned = empty_transposes("ss", tw)
+        dz1_nodes[0] = quantize("a0", turned_a, E5M2)
+        grouped = interleave_pairs(dz2)
+        wq[1, 0] = quantize("w10", turned, E4M3)
+        dz2q[1] = quantize("dz21", grouped, E5M2)
+        turned = empty_transposes("ss", tw2)
+        oa = dx_pair(0, 0)
+        ob = dx_pair(0, 1)
+        gb = interleave("v", dz1[0])
+        gx = interleave("v", x_raw[0])
+        round_dz1(1, m1, "ssss")
+        m2 = dh_x2(2)
+        dz1_chan[0] = quantize("b0", gb, E5M2)
+        xq[0] = quantize("x0", gx, E4M3)
+        wq[1, 1] = quantize("w11", turned, E4M3)
+        store_pair(oa, "ss", out0_view(0, 0))
+        ta = transposes(dz1[1], False)
+        store_pair(ob, "ss", out0_view(0, 1))
+        gb = interleave("v", dz1[1])
+        turned_a = empty_transposes("ss", ta)
+        ds = [take_bank(), take_bank(), take_bank(), take_bank()]
+
+        def ds_pass(i):
+            for s in (0, 2, 1, 3):
+                mx(ds[s], dz1_chan[i], s, xq[i], i == 0, i == 3)
+
+        ds_pass(0)
+        gx = interleave("v", x_raw[1])
+        dz1_nodes[1] = quantize("a1", turned_a, E5M2)
+        dz1_chan[1] = quantize("b1", gb, E5M2)
+        xq[1] = quantize("x1", gx, E4M3)
+        round_dz1(2, m2, "ssss")
+        oa = dx_pair(1, 0)
+        ta = transposes(dz1[2], False)
+        gx = interleave("v", x_raw[2])
+        gb = interleave("v", dz1[2])
+        store_pair(oa, "ss", out0_view(1, 0))
+        ob = dx_pair(1, 1)
+        turned_a = empty_transposes("ss", ta)
+        ds_pass(1)
+        dz1_nodes[2] = quantize("a2", turned_a, E5M2)
+        xq[2] = quantize("x2", gx, E4M3)
+        dz1_chan[2] = quantize("b2", gb, E5M2)
+        oa = dx_pair(2, 0)
+        store_pair(ob, "ss", out0_view(1, 1))
+        gx = interleave("v", x_raw[3])
+        m3 = dh_x2(3, (0, 1))
+        store_pair(oa, "ss", out0_view(2, 0))
+        m3 = m3 + dh_x2(3, (2, 3))
+        ds_pass(2)
+        xq[3] = quantize("x3", gx, E4M3)
+        round_dz1(3, m3, "svss")
+        ob = dx_pair(2, 1)
+        ta = transposes(dz1[3], False)
+        gb = interleave("v", dz1[3])
+        store_pair(ob, "ss", out0_view(2, 1))
+        turned_a = empty_transposes("ss", ta)
+        dz1_chan[3] = quantize("b3", gb, E5M2)
+        ds_pass(3)
+        dz1_nodes[3] = quantize("a3", turned_a, E5M2)
+        oa = dx_pair(3, 0)
+        ob = dx_pair(3, 1)
+        rows1 = out_1.rearrange("(h q e) m -> h q (e m)", h=2, e=2)
+        store_pair([ds[0], ds[2]], "sv", rows1[0])
+        store_pair([ds[1], ds[3]], "sv", rows1[1])
+        store_pair(oa, "sv", out0_view(3, 0), split=True)
+        store_pair(ob, "sv", out0_view(3, 1), split=True)

@@ -41,34 +41,37 @@ def tile_dcgrucell_pc_v_kernel(
             nc.sync.dma_start(out=raw[:], in_=view.rearrange("p j w -> p (j w)"))
             return raw
 
-        def load_gates(b):
-            tiles = []
-            for h in range(2):
-                tiles.append(
-                    (
-                        load("u%d%d" % (b, h), u[b], BF16, h),
-                        load("g%d%d" % (b, h), grad_out[b], BF16, h),
-                        load("c%d%d" % (b, h), cand[b], F32, h),
-                    )
-                )
-            return tiles
+        def load_gates(b, h):
+            return (
+                load("u%d%d" % (b, h), u[b], BF16, h),
+                load("g%d%d" % (b, h), grad_out[b], BF16, h),
+                load("c%d%d" % (b, h), cand[b], F32, h),
+            )
 
         def load_w(block, g):
             r0 = C * block + K * g
             return load("w%d%d" % (block, g), W_c[r0 : r0 + K, :], BF16)
 
         w_raw = {}
-        gates = [load_gates(0)]
+        units = [(b, g) for b in range(B) for g in range(C // K)]
+
+        def load_x(i):
+            b, g = units[i]
+            return load("x%d" % i, x1_0[b, K * g : K * (g + 1), :], BF16)
+
+        gates = {}
+        x_raw = {}
+        gates[0, 0] = load_gates(0, 0)
+        gates[0, 1] = load_gates(0, 1)
         w_raw[2, 0] = load_w(2, 0)
         w_raw[2, 1] = load_w(2, 1)
         sup_raw = load("sup", support0, BF16)
         w_raw[1, 0] = load_w(1, 0)
-        gates.append(load_gates(1))
+        gates[1, 0] = load_gates(1, 0)
+        gates[1, 1] = load_gates(1, 1)
         w_raw[1, 1] = load_w(1, 1)
-        units = [(b, g) for b in range(B) for g in range(C // K)]
-        x_raw = {}
         for i in range(4):
-            x_raw[i] = load("x%d" % i, x1_0[units[i][0], K * units[i][1] : K * units[i][1] + K, :], BF16)
+            x_raw[i] = load_x(i)
 
         ident0 = keep.tile([P, P], F32, name="ident0")
         make_identity(nc, ident0[:])
@@ -147,22 +150,29 @@ def tile_dcgrucell_pc_v_kernel(
                 banks.append(bank)
             return banks
 
-        def empty_transposes(engs, banks):
+        def new_turned():
             turned = work.tile([P, WIDE], BF16, name="turned", tag="turned", bufs=3, align_bytes=64)
+            return turned
+
+        def empty_bank(eng, turned, banks, pair):
             words = turned[:].bitcast(F32)
+            copy_on(
+                eng,
+                words[:, 512 * pair : 512 * (pair + 1)].rearrange("p (t c h) -> p t c h", t=2, h=2),
+                banks[pair][:].rearrange("p (t h c) -> p t c h", t=2, h=2),
+            )
+            give_bank(banks[pair])
+
+        def empty_transposes(engs, banks):
+            turned = new_turned()
             for pair in range(2):
-                copy_on(
-                    engs[pair],
-                    words[:, 512 * pair : 512 * (pair + 1)].rearrange("p (t c h) -> p t c h", t=2, h=2),
-                    banks[pair][:].rearrange("p (t h c) -> p t c h", t=2, h=2),
-                )
-                give_bank(banks[pair])
+                empty_bank(engs[pair], turned, banks, pair)
             return turned
 
         def gate_product(b, h):
             a = work.tile([P, 1024], F32, name="a", tag="a")
             nc.vector.scalar_tensor_tensor(
-                out=a[:], in0=gates[b][h][0][:], scalar=1.0, in1=gates[b][h][1][:], op0=ALU.subtract, op1=ALU.mult
+                out=a[:], in0=gates[b, h][0][:], scalar=1.0, in1=gates[b, h][1][:], op0=ALU.subtract, op1=ALU.mult
             )
             return a
 
@@ -170,7 +180,7 @@ def tile_dcgrucell_pc_v_kernel(
             s = work.tile([P, 1024], F32, name="s", tag="s")
             nc.scalar.activation(
                 out=s[:].rearrange("p (n e) -> p n e", e=2),
-                in_=gates[b][h][2][:].rearrange("p (e n) -> p n e", e=2),
+                in_=gates[b, h][2][:].rearrange("p (e n) -> p n e", e=2),
                 func=ACT.Square,
             )
             return s
@@ -209,16 +219,30 @@ def tile_dcgrucell_pc_v_kernel(
                 banks.append(bank)
             return banks
 
-        def round_dz1(i, banks, engs):
-            dz1[i] = keep.tile([P, WIDE], BF16, name="dz1_%d" % i, align_bytes=64)
-            for t in range(PACK):
+        def round_dz1(i, banks, engs, slots=range(PACK)):
+            if i not in dz1:
+                dz1[i] = keep.tile([P, WIDE], BF16, name="dz1_%d" % i, align_bytes=64)
+            for k, t in enumerate(slots):
                 out = dz1[i][:, 512 * t : 512 * (t + 1)].rearrange("p (h q) -> p h q", h=2)
-                in_ = banks[t][:].rearrange("p (q h) -> p h q", h=2)
-                if engs[t] == "s":
+                in_ = banks[k][:].rearrange("p (q h) -> p h q", h=2)
+                if engs[k] == "s":
                     nc.scalar.activation(out=out, in_=in_, func=ACT.Copy, scale=2.0)
                 else:
                     nc.vector.tensor_scalar(out=out, in0=in_, scalar1=2.0, scalar2=None, op0=ALU.mult)
-                give_bank(banks[t])
+                give_bank(banks[k])
+
+        def dx_open(i, pair):
+            b, g = units[i]
+            banks = []
+            for t in (2 * pair, 2 * pair + 1):
+                bank = take_bank()
+                mx(bank, wq[1, g], t, dz2q[b], True, False)
+                banks.append(bank)
+            return banks
+
+        def dx_close(i, pair, banks):
+            for k in range(2):
+                mx(banks[k], dz1_nodes[i], 2 * pair + k, supq, False, True)
 
         def dx_pair(i, pair):
             b, g = units[i]
@@ -231,7 +255,7 @@ def tile_dcgrucell_pc_v_kernel(
             return banks
 
         def store_pair(banks, engs, dst, split=False):
-            res = work.tile([P, 1024], F32, name="res", tag="res", bufs=5)
+            res = work.tile([P, 1024], F32, name="res", tag="res", bufs=4)
             for k in range(2):
                 copy_on(engs[k], res[:, 512 * k : 512 * (k + 1)], banks[k][:])
                 give_bank(banks[k])
@@ -239,6 +263,30 @@ def tile_dcgrucell_pc_v_kernel(
                     nc.sync.dma_start(out=dst[:, 512 * k : 512 * (k + 1)], in_=res[:, 512 * k : 512 * (k + 1)])
             if not split:
                 nc.sync.dma_start(out=dst, in_=res[:])
+
+        def store_one(bank, eng, dst):
+            res1 = work.tile([P, 512], F32, name="res1", tag="res1", bufs=8)
+            copy_on(eng, res1[:], bank[:])
+            give_bank(bank)
+            nc.sync.dma_start(out=dst, in_=res1[:])
+
+        def interleave_half(raw, grouped, h):
+            nc.vector.tensor_copy(
+                out=grouped[:, 1024 * h : 1024 * (h + 1)].rearrange("p (c i t) -> p c t i", i=4, t=PACK),
+                in_=raw[:].rearrange("p (t h c i) -> p h c t i", i=4, t=PACK, h=2)[:, h],
+            )
+
+        def quantize_half(q, grouped, h):
+            nc.vector.quantize_mx(
+                out=q[0][:, 256 * h : 256 * (h + 1)].bitcast(q[2]),
+                scales=q[1][:, 256 * h : 256 * (h + 1)],
+                in_=grouped[:, 1024 * h : 1024 * (h + 1)],
+            )
+
+        def new_codes(name, fmt):
+            codes = keep.tile([P, 512], U32, name=name + "_codes", align_bytes=64)
+            scales = keep.tile([P, 512], U8, name=name + "_scales", align_bytes=64)
+            return (codes, scales, fmt)
 
         def out0_view(i, pair):
             b, g = units[i]
@@ -267,79 +315,89 @@ def tile_dcgrucell_pc_v_kernel(
         tw = transposes(w_raw[1, 0], True)
         round_dz1(0, m0, "ssss")
         ta = transposes(dz1[0], False)
+        m1 = dh_x2(1)
         a1 = gate_product(1, 1)
+        turned = empty_transposes("ss", tw)
+        tw = transposes(w_raw[1, 1], True)
+        gb = interleave("v", dz1[0])
+        turned_a = empty_transposes("ss", ta)
+        wq[1, 0] = quantize("w10", turned, E4M3)
+        dz1_nodes[0] = quantize("a0", turned_a, E5M2)
+        oa = dx_pair(0, 0)
+        dz1_chan[0] = quantize("b0", gb, E5M2)
         s0 = square(1, 0)
         s1 = square(1, 1)
-        m1 = dh_x2(1)
         dz2 = work.tile([P, WIDE], BF16, name="dz2", tag="dz2")
         dz2_half(dz2, 0, s0, a0)
         dz2_half(dz2, 1, s1, a1)
-        turned_a = empty_transposes("ss", ta)
-        tw2 = transposes(w_raw[1, 1], True)
-        turned = empty_transposes("ss", tw)
-        dz1_nodes[0] = quantize("a0", turned_a, E5M2)
-        grouped = interleave_pairs(dz2)
-        wq[1, 0] = quantize("w10", turned, E4M3)
-        dz2q[1] = quantize("dz21", grouped, E5M2)
-        turned = empty_transposes("ss", tw2)
-        oa = dx_pair(0, 0)
-        ob = dx_pair(0, 1)
-        gb = interleave("v", dz1[0])
-        gx = interleave("v", x_raw[0])
         round_dz1(1, m1, "ssss")
-        m2 = dh_x2(2)
-        dz1_chan[0] = quantize("b0", gb, E5M2)
-        xq[0] = quantize("x0", gx, E4M3)
-        wq[1, 1] = quantize("w11", turned, E4M3)
-        store_pair(oa, "ss", out0_view(0, 0))
+        ob = dx_pair(0, 1)
         ta = transposes(dz1[1], False)
-        store_pair(ob, "ss", out0_view(0, 1))
-        gb = interleave("v", dz1[1])
+        gx = interleave("v", x_raw[0])
+        grouped = interleave_pairs(dz2)
+        xq[0] = quantize("x0", gx, E4M3)
+        dz2q[1] = quantize("dz21", grouped, E5M2)
+        turned = empty_transposes("ss", tw)
         turned_a = empty_transposes("ss", ta)
         ds = [take_bank(), take_bank(), take_bank(), take_bank()]
 
-        def ds_pass(i):
-            for s in (0, 2, 1, 3):
+        def ds_pass(i, slices=(0, 1, 2, 3)):
+            for s in slices:
                 mx(ds[s], dz1_chan[i], s, xq[i], i == 0, i == 3)
 
         ds_pass(0)
+        gb = interleave("v", dz1[1])
         gx = interleave("v", x_raw[1])
-        dz1_nodes[1] = quantize("a1", turned_a, E5M2)
         dz1_chan[1] = quantize("b1", gb, E5M2)
         xq[1] = quantize("x1", gx, E4M3)
+        wq[1, 1] = quantize("w11", turned, E4M3)
+        dz1_nodes[1] = quantize("a1", turned_a, E5M2)
+        store_pair(oa, "ss", out0_view(0, 0))
+        store_pair(ob, "ss", out0_view(0, 1))
+        m2 = dh_x2(2)
         round_dz1(2, m2, "ssss")
-        oa = dx_pair(1, 0)
+        m3 = dh_x2(3, (0, 1))
+        ds_pass(1)
         ta = transposes(dz1[2], False)
         gx = interleave("v", x_raw[2])
+        round_dz1(3, m3, "ss", (0, 1))
+        m3 = dh_x2(3, (2, 3))
+        turned_a = empty_transposes("ss", ta)
+        xq[2] = quantize("x2", gx, E4M3)
+        round_dz1(3, m3, "vv", (2, 3))
+        oa = dx_pair(1, 0)
+        ta = transposes(dz1[3], False)
         gb = interleave("v", dz1[2])
+        dz1_nodes[2] = quantize("a2", turned_a, E5M2)
+        dz1_chan[2] = quantize("b2", gb, E5M2)
         store_pair(oa, "ss", out0_view(1, 0))
         ob = dx_pair(1, 1)
         turned_a = empty_transposes("ss", ta)
-        ds_pass(1)
-        dz1_nodes[2] = quantize("a2", turned_a, E5M2)
-        xq[2] = quantize("x2", gx, E4M3)
-        dz1_chan[2] = quantize("b2", gb, E5M2)
         oa = dx_pair(2, 0)
-        store_pair(ob, "ss", out0_view(1, 1))
         gx = interleave("v", x_raw[3])
-        m3 = dh_x2(3, (0, 1))
-        store_pair(oa, "ss", out0_view(2, 0))
-        m3 = m3 + dh_x2(3, (2, 3))
-        ds_pass(2)
-        xq[3] = quantize("x3", gx, E4M3)
-        round_dz1(3, m3, "svss")
-        ob = dx_pair(2, 1)
-        ta = transposes(dz1[3], False)
-        gb = interleave("v", dz1[3])
-        store_pair(ob, "ss", out0_view(2, 1))
-        turned_a = empty_transposes("ss", ta)
-        dz1_chan[3] = quantize("b3", gb, E5M2)
-        ds_pass(3)
         dz1_nodes[3] = quantize("a3", turned_a, E5M2)
+        xq[3] = quantize("x3", gx, E4M3)
+        gb = work.tile([P, WIDE], BF16, name="grouped", tag="grouped", bufs=3, align_bytes=64)
+        dz1_chan[3] = new_codes("b3", E5M2)
+        interleave_half(dz1[3], gb, 0)
+        interleave_half(dz1[3], gb, 1)
+        quantize_half(dz1_chan[3], gb, 0)
+        quantize_half(dz1_chan[3], gb, 1)
+        store_pair(ob, "ss", out0_view(1, 1), split=True)
+        ob = dx_pair(2, 1)
+        store_pair(oa, "ss", out0_view(2, 0))
         oa = dx_pair(3, 0)
+        store_pair(ob, "ss", out0_view(2, 1))
         ob = dx_pair(3, 1)
-        rows1 = out_1.rearrange("(h q e) m -> h q (e m)", h=2, e=2)
-        store_pair([ds[0], ds[2]], "sv", rows1[0])
-        store_pair([ds[1], ds[3]], "sv", rows1[1])
-        store_pair(oa, "sv", out0_view(3, 0), split=True)
-        store_pair(ob, "sv", out0_view(3, 1), split=True)
+        for s in range(4):
+            ds_pass(2, (s,))
+            ds_pass(3, (s,))
+        rows0 = out_0[1, K : 2 * K, :].rearrange("(p t) m -> t p m", t=PACK)
+        rows1 = out_1.rearrange("(h q e) m -> e h q m", h=2, e=2)
+        store_pair(oa, "ss", out0_view(3, 0))
+        store_one(ob[0], "v", rows0[2])
+        store_one(ob[1], "s", rows0[3])
+        store_one(ds[0], "v", rows1[0, 0])
+        store_one(ds[1], "s", rows1[0, 1])
+        store_one(ds[2], "v", rows1[1, 0])
+        store_one(ds[3], "s", rows1[1, 1])

@@ -41,11 +41,12 @@ def tile_dcgrucell_pc_v_kernel(
             nc.sync.dma_start(out=raw[:], in_=view.rearrange("p j w -> p (j w)"))
             return raw
 
-        def load_gates(b, h):
+        def load_gates(b):
             return (
-                load("u%d%d" % (b, h), u[b], BF16, h),
-                load("g%d%d" % (b, h), grad_out[b], BF16, h),
-                load("c%d%d" % (b, h), cand[b], F32, h),
+                load("u%d" % b, u[b], BF16),
+                load("g%d" % b, grad_out[b], BF16),
+                load("c%d0" % b, cand[b], F32, 0),
+                load("c%d1" % b, cand[b], F32, 1),
             )
 
         def load_w(block, g):
@@ -61,14 +62,14 @@ def tile_dcgrucell_pc_v_kernel(
 
         gates = {}
         x_raw = {}
-        gates[0, 0] = load_gates(0, 0)
-        gates[0, 1] = load_gates(0, 1)
-        w_raw[2, 0] = load_w(2, 0)
+        ug0 = (load("u0", u[0], BF16), load("g0", grad_out[0], BF16), load("c00", cand[0], F32, 0))
+        w_first = [load("w20a", W_c[2 * C : 2 * C + K, :], BF16, 0)]
+        gates[0] = ug0 + (load("c01", cand[0], F32, 1),)
+        w_first.append(load("w20b", W_c[2 * C : 2 * C + K, :], BF16, 1))
         w_raw[2, 1] = load_w(2, 1)
         sup_raw = load("sup", support0, BF16)
         w_raw[1, 0] = load_w(1, 0)
-        gates[1, 0] = load_gates(1, 0)
-        gates[1, 1] = load_gates(1, 1)
+        gates[1] = load_gates(1)
         w_raw[1, 1] = load_w(1, 1)
         for i in range(4):
             x_raw[i] = load_x(i)
@@ -133,11 +134,17 @@ def tile_dcgrucell_pc_v_kernel(
             )
             return grouped
 
-        def transposes(src, stepped):
+        def keep_warm(bank, passes):
+            for k in range(passes):
+                mx(bank, wq[2, 0], 0, dz2q[0], True, True)
+
+        def transposes(src, stepped, warm=0):
             words = src[:].bitcast(F32)
             banks = []
             for pair in range(2):
                 bank = take_bank()
+                if pair == 0:
+                    keep_warm(bank, warm)
                 for t2 in range(2):
                     for h in range(2):
                         w0 = 256 * (2 * pair + t2)
@@ -149,6 +156,17 @@ def tile_dcgrucell_pc_v_kernel(
                         nc.tensor.transpose(bank[:, P * slot : P * (slot + 1)], in_, ident[:])
                 banks.append(bank)
             return banks
+
+        def transpose_half(src):
+            words = src[:].bitcast(F32)
+            bank = take_bank()
+            for t2 in range(2):
+                for h in range(2):
+                    slot = 2 * t2 + h
+                    nc.tensor.transpose(
+                        bank[:, P * slot : P * (slot + 1)], words[:, 256 * t2 + h : 256 * (t2 + 1) : 2], ident[:]
+                    )
+            return bank
 
         def new_turned():
             turned = work.tile([P, WIDE], BF16, name="turned", tag="turned", bufs=3, align_bytes=64)
@@ -172,7 +190,7 @@ def tile_dcgrucell_pc_v_kernel(
         def gate_product(b, h):
             a = work.tile([P, 1024], F32, name="a", tag="a")
             nc.vector.scalar_tensor_tensor(
-                out=a[:], in0=gates[b, h][0][:], scalar=1.0, in1=gates[b, h][1][:], op0=ALU.subtract, op1=ALU.mult
+                out=a[:], in0=gates[b][0][:, 1024 * h : 1024 * (h + 1)], scalar=1.0, in1=gates[b][1][:, 1024 * h : 1024 * (h + 1)], op0=ALU.subtract, op1=ALU.mult
             )
             return a
 
@@ -180,7 +198,7 @@ def tile_dcgrucell_pc_v_kernel(
             s = work.tile([P, 1024], F32, name="s", tag="s")
             nc.scalar.activation(
                 out=s[:].rearrange("p (n e) -> p n e", e=2),
-                in_=gates[b, h][2][:].rearrange("p (e n) -> p n e", e=2),
+                in_=gates[b][2 + h][:].rearrange("p (e n) -> p n e", e=2),
                 func=ACT.Square,
             )
             return s
@@ -203,6 +221,29 @@ def tile_dcgrucell_pc_v_kernel(
             )
             return grouped
 
+        def square_cols(s, b, h, n0):
+            nc.scalar.activation(
+                out=s[:].rearrange("p (n e) -> p n e", e=2)[:, n0 : n0 + 256, :],
+                in_=gates[b][2 + h][:].rearrange("p (e n) -> p n e", e=2)[:, n0 : n0 + 256, :],
+                func=ACT.Square,
+            )
+
+        def dz2_cols(dz2, h, s, a, n0):
+            nc.vector.scalar_tensor_tensor(
+                out=dz2[:, 1024 * h : 1024 * (h + 1)].rearrange("p (n e) -> p n e", e=2)[:, n0 : n0 + 256, :],
+                in0=s[:].rearrange("p (n e) -> p n e", e=2)[:, n0 : n0 + 256, :],
+                scalar=1.0,
+                in1=a[:].rearrange("p (e n) -> p n e", e=2)[:, n0 : n0 + 256, :],
+                op0=ALU.subtract,
+                op1=ALU.mult,
+            )
+
+        def pairs_cols(grouped, dz2, n0):
+            nc.vector.tensor_copy(
+                out=grouped[:].bitcast(F32).rearrange("p (n h) -> p n h", h=2)[:, n0 : n0 + 256, :],
+                in_=dz2[:].bitcast(F32).rearrange("p (h n) -> p n h", h=2)[:, n0 : n0 + 256, :],
+            )
+
         wq = {}
         dz2q = {}
         dz1 = {}
@@ -210,13 +251,14 @@ def tile_dcgrucell_pc_v_kernel(
         dz1_chan = {}
         xq = {}
 
-        def dh_x2(i, slots=range(PACK)):
+        def dh_x2(i, slots=range(PACK), warm=0):
             b, g = units[i]
             banks = []
             for t in slots:
-                bank = take_bank()
-                mx(bank, wq[2, g], t, dz2q[b], True, True)
-                banks.append(bank)
+                banks.append(take_bank())
+                keep_warm(banks[-1], warm)
+            for k, t in enumerate(slots):
+                mx(banks[k], wq[2, g], t, dz2q[b], True, True)
             return banks
 
         def round_dz1(i, banks, engs, slots=range(PACK)):
@@ -244,18 +286,20 @@ def tile_dcgrucell_pc_v_kernel(
             for k in range(2):
                 mx(banks[k], dz1_nodes[i], 2 * pair + k, supq, False, True)
 
-        def dx_pair(i, pair):
+        def dx_pair(i, pair, warm=0):
             b, g = units[i]
             banks = []
             for t in (2 * pair, 2 * pair + 1):
                 bank = take_bank()
+                if t == 2 * pair:
+                    keep_warm(bank, warm)
                 mx(bank, wq[1, g], t, dz2q[b], True, False)
                 mx(bank, dz1_nodes[i], t, supq, False, True)
                 banks.append(bank)
             return banks
 
         def store_pair(banks, engs, dst, split=False):
-            res = work.tile([P, 1024], F32, name="res", tag="res", bufs=4)
+            res = work.tile([P, 1024], F32, name="res", tag="res", bufs=6)
             for k in range(2):
                 copy_on(engs[k], res[:, 512 * k : 512 * (k + 1)], banks[k][:])
                 give_bank(banks[k])
@@ -293,38 +337,63 @@ def tile_dcgrucell_pc_v_kernel(
             rows = out_0[b, K * g : K * (g + 1), :].rearrange("(p t) m -> p (t m)", t=PACK)
             return rows[:, 1024 * pair : 1024 * (pair + 1)]
 
+        warm_mov = quantize("warm_mov", gates[0][0], E4M3)
+        warm_stat = new_codes("warm_stat", E5M2)
+        nc.vector.quantize_mx(out=warm_stat[0][:, 0:P].bitcast(E5M2), scales=warm_stat[1][:, 0:P], in_=gates[0][0][:, 0:512])
+        warm_bank = take_bank()
+
+        def warm_up(passes):
+            for k in range(passes):
+                mx(warm_bank, warm_stat, 0, warm_mov, True, True)
+
+        warm_up(4)
         a0 = gate_product(0, 0)
-        s0 = square(0, 0)
         a1 = gate_product(0, 1)
-        s1 = square(0, 1)
+        s0 = square(0, 0)
         dz2 = work.tile([P, WIDE], BF16, name="dz2", tag="dz2")
         dz2_half(dz2, 0, s0, a0)
-        dz2_half(dz2, 1, s1, a1)
-        tw = transposes(w_raw[2, 0], True)
-        turned = empty_transposes("ss", tw)
-        grouped = interleave_pairs(dz2)
+        tw = [transpose_half(w_first[0])]
+        warm_up(3)
+        tw.append(transpose_half(w_first[1]))
+        warm_up(2)
+        s1 = work.tile([P, 1024], F32, name="s", tag="s")
+        turned = new_turned()
+        square_cols(s1, 0, 1, 0)
+        square_cols(s1, 0, 1, 256)
+        empty_bank("s", turned, tw, 0)
+        empty_bank("s", turned, tw, 1)
+        dz2_cols(dz2, 1, s1, a1, 0)
+        dz2_cols(dz2, 1, s1, a1, 256)
+        grouped = work.tile([P, WIDE], BF16, name="grouped", tag="grouped", bufs=3, align_bytes=64)
+        wq[2, 0] = new_codes("w20", E4M3)
+        dz2q[0] = new_codes("dz20", E5M2)
+        pairs_cols(grouped, dz2, 0)
+        quantize_half(wq[2, 0], turned, 0)
+        pairs_cols(grouped, dz2, 256)
+        quantize_half(dz2q[0], grouped, 0)
+        quantize_half(dz2q[0], grouped, 1)
+        quantize_half(wq[2, 0], turned, 1)
         tw = transposes(w_raw[2, 1], True)
-        dz2q[0] = quantize("dz20", grouped, E5M2)
-        wq[2, 0] = quantize("w20", turned, E4M3)
+        warm_up(2)
+        give_bank(warm_bank)
         m0 = dh_x2(0)
         turned = empty_transposes("ss", tw)
         sup_g = interleave_support("v", sup_raw)
-        a0 = gate_product(1, 0)
         wq[2, 1] = quantize("w21", turned, E4M3)
         supq = quantize("sup", sup_g, E4M3)
+        a0 = gate_product(1, 0)
         tw = transposes(w_raw[1, 0], True)
         round_dz1(0, m0, "ssss")
-        ta = transposes(dz1[0], False)
+        ta = transposes(dz1[0], False, 2)
         m1 = dh_x2(1)
         a1 = gate_product(1, 1)
         turned = empty_transposes("ss", tw)
-        tw = transposes(w_raw[1, 1], True)
+        tw = transposes(w_raw[1, 1], True, 3)
         gb = interleave("v", dz1[0])
         turned_a = empty_transposes("ss", ta)
         wq[1, 0] = quantize("w10", turned, E4M3)
         dz1_nodes[0] = quantize("a0", turned_a, E5M2)
-        oa = dx_pair(0, 0)
-        dz1_chan[0] = quantize("b0", gb, E5M2)
+        oa = dx_pair(0, 0, 0)
         s0 = square(1, 0)
         s1 = square(1, 1)
         dz2 = work.tile([P, WIDE], BF16, name="dz2", tag="dz2")
@@ -333,19 +402,14 @@ def tile_dcgrucell_pc_v_kernel(
         round_dz1(1, m1, "ssss")
         ob = dx_pair(0, 1)
         ta = transposes(dz1[1], False)
-        gx = interleave("v", x_raw[0])
+        dz1_chan[0] = quantize("b0", gb, E5M2)
         grouped = interleave_pairs(dz2)
-        xq[0] = quantize("x0", gx, E4M3)
+        gx = interleave("v", x_raw[0])
         dz2q[1] = quantize("dz21", grouped, E5M2)
+        xq[0] = quantize("x0", gx, E4M3)
         turned = empty_transposes("ss", tw)
         turned_a = empty_transposes("ss", ta)
-        ds = [take_bank(), take_bank(), take_bank(), take_bank()]
-
-        def ds_pass(i, slices=(0, 1, 2, 3)):
-            for s in slices:
-                mx(ds[s], dz1_chan[i], s, xq[i], i == 0, i == 3)
-
-        ds_pass(0)
+        m2 = dh_x2(2, warm=1)
         gb = interleave("v", dz1[1])
         gx = interleave("v", x_raw[1])
         dz1_chan[1] = quantize("b1", gb, E5M2)
@@ -354,21 +418,27 @@ def tile_dcgrucell_pc_v_kernel(
         dz1_nodes[1] = quantize("a1", turned_a, E5M2)
         store_pair(oa, "ss", out0_view(0, 0))
         store_pair(ob, "ss", out0_view(0, 1))
-        m2 = dh_x2(2)
+        ds = [take_bank(), take_bank(), take_bank(), take_bank()]
+
+        def ds_pass(i, slices=(0, 2, 1, 3)):
+            for s in slices:
+                mx(ds[s], dz1_chan[i], s, xq[i], i == 0, i == 3)
+
+        ds_pass(0, (0, 1, 2, 3))
         round_dz1(2, m2, "ssss")
         m3 = dh_x2(3, (0, 1))
-        ds_pass(1)
-        ta = transposes(dz1[2], False)
+        ta = transposes(dz1[2], False, 1)
         gx = interleave("v", x_raw[2])
         round_dz1(3, m3, "ss", (0, 1))
         m3 = dh_x2(3, (2, 3))
+        ds_pass(1)
         turned_a = empty_transposes("ss", ta)
-        xq[2] = quantize("x2", gx, E4M3)
-        round_dz1(3, m3, "vv", (2, 3))
+        gb = interleave("v", dz1[2])
+        round_dz1(3, m3, "ss", (2, 3))
         oa = dx_pair(1, 0)
         ta = transposes(dz1[3], False)
-        gb = interleave("v", dz1[2])
         dz1_nodes[2] = quantize("a2", turned_a, E5M2)
+        xq[2] = quantize("x2", gx, E4M3)
         dz1_chan[2] = quantize("b2", gb, E5M2)
         store_pair(oa, "ss", out0_view(1, 0))
         ob = dx_pair(1, 1)
@@ -376,28 +446,20 @@ def tile_dcgrucell_pc_v_kernel(
         oa = dx_pair(2, 0)
         gx = interleave("v", x_raw[3])
         dz1_nodes[3] = quantize("a3", turned_a, E5M2)
+        gb = interleave("v", dz1[3])
         xq[3] = quantize("x3", gx, E4M3)
-        gb = work.tile([P, WIDE], BF16, name="grouped", tag="grouped", bufs=3, align_bytes=64)
-        dz1_chan[3] = new_codes("b3", E5M2)
-        interleave_half(dz1[3], gb, 0)
-        interleave_half(dz1[3], gb, 1)
-        quantize_half(dz1_chan[3], gb, 0)
-        quantize_half(dz1_chan[3], gb, 1)
-        store_pair(ob, "ss", out0_view(1, 1), split=True)
+        dz1_chan[3] = quantize("b3", gb, E5M2)
+        store_pair(ob, "ss", out0_view(1, 1))
         ob = dx_pair(2, 1)
         store_pair(oa, "ss", out0_view(2, 0))
         oa = dx_pair(3, 0)
         store_pair(ob, "ss", out0_view(2, 1))
         ob = dx_pair(3, 1)
-        for s in range(4):
+        for s in (0, 2, 1, 3):
             ds_pass(2, (s,))
             ds_pass(3, (s,))
-        rows0 = out_0[1, K : 2 * K, :].rearrange("(p t) m -> t p m", t=PACK)
-        rows1 = out_1.rearrange("(h q e) m -> e h q m", h=2, e=2)
+        rows1 = out_1.rearrange("(h q e) m -> h q (e m)", h=2, e=2)
         store_pair(oa, "ss", out0_view(3, 0))
-        store_one(ob[0], "v", rows0[2])
-        store_one(ob[1], "s", rows0[3])
-        store_one(ds[0], "v", rows1[0, 0])
-        store_one(ds[1], "s", rows1[0, 1])
-        store_one(ds[2], "v", rows1[1, 0])
-        store_one(ds[3], "s", rows1[1, 1])
+        store_pair(ob, "vs", out0_view(3, 1))
+        store_pair([ds[0], ds[2]], "vs", rows1[0])
+        store_pair([ds[1], ds[3]], "vs", rows1[1], split=True)

@@ -125,12 +125,12 @@ def tile_dcgrucell_pc_v_kernel(
             )
             return grouped
 
-        def interleave_support(eng, raw):
+        def interleave_dz1(eng, raw):
             grouped = work.tile([P, WIDE], BF16, name="grouped", tag="grouped", bufs=3, align_bytes=64)
             copy_on(
                 eng,
-                grouped[:].rearrange("p (c i u e) -> p c u e i", i=4, u=2, e=2),
-                raw[:].rearrange("p (e u c i) -> p c u e i", i=4, u=2, e=2),
+                grouped[:].rearrange("p (w h e t) -> p h w t e", h=2, e=2, t=PACK),
+                raw[:].rearrange("p (t h w e) -> p h w t e", h=2, e=2, t=PACK),
             )
             return grouped
 
@@ -265,8 +265,8 @@ def tile_dcgrucell_pc_v_kernel(
             if i not in dz1:
                 dz1[i] = keep.tile([P, WIDE], BF16, name="dz1_%d" % i, align_bytes=64)
             for k, t in enumerate(slots):
-                out = dz1[i][:, 512 * t : 512 * (t + 1)].rearrange("p (h q) -> p h q", h=2)
-                in_ = banks[k][:].rearrange("p (q h) -> p h q", h=2)
+                out = dz1[i][:, 512 * t : 512 * (t + 1)].rearrange("p (h w e) -> p h w e", h=2, e=2)
+                in_ = banks[k][:].rearrange("p (w h e) -> p h w e", h=2, e=2)
                 if engs[k] == "s":
                     nc.scalar.activation(out=out, in_=in_, func=ACT.Copy, scale=2.0)
                 else:
@@ -304,9 +304,9 @@ def tile_dcgrucell_pc_v_kernel(
                 copy_on(engs[k], res[:, 512 * k : 512 * (k + 1)], banks[k][:])
                 give_bank(banks[k])
                 if split:
-                    nc.sync.dma_start(out=dst[:, 512 * k : 512 * (k + 1)], in_=res[:, 512 * k : 512 * (k + 1)])
+                    nc.sync.dma_start(out=dst[:, k, :], in_=res[:, 512 * k : 512 * (k + 1)])
             if not split:
-                nc.sync.dma_start(out=dst, in_=res[:])
+                nc.sync.dma_start(out=dst, in_=res[:].rearrange("p (k m) -> p k m", k=2))
 
         def store_one(bank, eng, dst):
             res1 = work.tile([P, 512], F32, name="res1", tag="res1", bufs=8)
@@ -334,8 +334,8 @@ def tile_dcgrucell_pc_v_kernel(
 
         def out0_view(i, pair):
             b, g = units[i]
-            rows = out_0[b, K * g : K * (g + 1), :].rearrange("(p t) m -> p (t m)", t=PACK)
-            return rows[:, 1024 * pair : 1024 * (pair + 1)]
+            rows = out_0[b, K * g : K * (g + 1), :].rearrange("(p t) m -> p t m", t=PACK)
+            return rows[:, 2 * pair : 2 * pair + 2, :]
 
         warm_mov = quantize("warm_mov", gates[0][0], E4M3)
         warm_stat = new_codes("warm_stat", E5M2)
@@ -378,7 +378,7 @@ def tile_dcgrucell_pc_v_kernel(
         give_bank(warm_bank)
         m0 = dh_x2(0)
         turned = empty_transposes("ss", tw)
-        sup_g = interleave_support("v", sup_raw)
+        sup_g = interleave("v", sup_raw)
         wq[2, 1] = quantize("w21", turned, E4M3)
         supq = quantize("sup", sup_g, E4M3)
         a0 = gate_product(1, 0)
@@ -389,7 +389,7 @@ def tile_dcgrucell_pc_v_kernel(
         a1 = gate_product(1, 1)
         turned = empty_transposes("ss", tw)
         tw = transposes(w_raw[1, 1], True, 3)
-        gb = interleave("v", dz1[0])
+        gb = interleave_dz1("v", dz1[0])
         turned_a = empty_transposes("ss", ta)
         wq[1, 0] = quantize("w10", turned, E4M3)
         dz1_nodes[0] = quantize("a0", turned_a, E5M2)
@@ -410,7 +410,7 @@ def tile_dcgrucell_pc_v_kernel(
         turned = empty_transposes("ss", tw)
         turned_a = empty_transposes("ss", ta)
         m2 = dh_x2(2, warm=1)
-        gb = interleave("v", dz1[1])
+        gb = interleave_dz1("v", dz1[1])
         gx = interleave("v", x_raw[1])
         dz1_chan[1] = quantize("b1", gb, E5M2)
         xq[1] = quantize("x1", gx, E4M3)
@@ -420,7 +420,7 @@ def tile_dcgrucell_pc_v_kernel(
         store_pair(ob, "ss", out0_view(0, 1))
         ds = [take_bank(), take_bank(), take_bank(), take_bank()]
 
-        def ds_pass(i, slices=(0, 2, 1, 3)):
+        def ds_pass(i, slices=(0, 1, 2, 3)):
             for s in slices:
                 mx(ds[s], dz1_chan[i], s, xq[i], i == 0, i == 3)
 
@@ -433,7 +433,7 @@ def tile_dcgrucell_pc_v_kernel(
         m3 = dh_x2(3, (2, 3))
         ds_pass(1)
         turned_a = empty_transposes("ss", ta)
-        gb = interleave("v", dz1[2])
+        gb = interleave_dz1("v", dz1[2])
         round_dz1(3, m3, "ss", (2, 3))
         oa = dx_pair(1, 0)
         ta = transposes(dz1[3], False)
@@ -446,7 +446,7 @@ def tile_dcgrucell_pc_v_kernel(
         oa = dx_pair(2, 0)
         gx = interleave("v", x_raw[3])
         dz1_nodes[3] = quantize("a3", turned_a, E5M2)
-        gb = interleave("v", dz1[3])
+        gb = interleave_dz1("v", dz1[3])
         xq[3] = quantize("x3", gx, E4M3)
         dz1_chan[3] = quantize("b3", gb, E5M2)
         store_pair(ob, "ss", out0_view(1, 1))
@@ -455,11 +455,11 @@ def tile_dcgrucell_pc_v_kernel(
         oa = dx_pair(3, 0)
         store_pair(ob, "ss", out0_view(2, 1))
         ob = dx_pair(3, 1)
-        for s in (0, 2, 1, 3):
+        for s in (0, 1, 2, 3):
             ds_pass(2, (s,))
             ds_pass(3, (s,))
-        rows1 = out_1.rearrange("(h q e) m -> h q (e m)", h=2, e=2)
+        rows1 = out_1.rearrange("(h k p) m -> h p k m", h=2, k=2)
         store_pair(oa, "ss", out0_view(3, 0))
         store_pair(ob, "vs", out0_view(3, 1))
-        store_pair([ds[0], ds[2]], "vs", rows1[0])
-        store_pair([ds[1], ds[3]], "vs", rows1[1], split=True)
+        store_pair([ds[0], ds[1]], "vs", rows1[0])
+        store_pair([ds[2], ds[3]], "vs", rows1[1], split=True)

from contextlib import ExitStack

import concourse.mybir as mybir
from concourse.masks import make_identity

B, HID, N, C = 2, 512, 512, 1024
FLOPS = 2 * B * 2 * C * HID * N + 2 * B * C * N * N + 2 * B * C * N * N
BYTES = 2 * (2 * B * HID * N + 2 * C * HID + N * N + B * C * N) + 4 * (B * HID * N + B * C * N + N * N)

F32 = mybir.dt.float32
BF16 = mybir.dt.bfloat16
U32 = mybir.dt.uint32
U8 = mybir.dt.uint8
E4M3 = mybir.dt.float8_e4m3fn_x4
E5M2 = mybir.dt.float8_e5m2_x4
ALU = mybir.AluOpType
ACT = mybir.ActivationFunctionType

P = 128
PACK = 4
K = P * PACK
WIDE = PACK * 512


def tile_dcgrucell_pc_v_kernel(
    tc, x_cand, x1_0, x1_1, support0, support1, W_c, b_c, u, hx, cand, grad_out, out_0, out_1
):
    nc = tc.nc
    with ExitStack() as ctx:
        keep = ctx.enter_context(tc.tile_pool(name="keep", bufs=1))
        work = ctx.enter_context(tc.tile_pool(name="work", bufs=2))
        psum = ctx.enter_context(tc.psum_pool(name="psum", bufs=1))
        ctx.enter_context(tc.manual_schedule())

        def load(name, rows, dtype, half=None):
            view = rows.rearrange("(p j) w -> p j w", j=PACK)
            if half is not None:
                view = view[:, 2 * half : 2 * half + 2, :]
            width = view.shape[1] * view.shape[2]
            raw = keep.tile([P, width], dtype, name=name, align_bytes=64)
            nc.sync.dma_start(out=raw[:], in_=view.rearrange("p j w -> p (j w)"))
            return raw

        def load_gates(b):
            return (
                load("u%d" % b, u[b], BF16),
                load("g%d" % b, grad_out[b], BF16),
                load("c%d0" % b, cand[b], F32, 0),
                load("c%d1" % b, cand[b], F32, 1),
            )

        def load_w(block, g):
            r0 = C * block + K * g
            return load("w%d%d" % (block, g), W_c[r0 : r0 + K, :], BF16)

        w_raw = {}
        units = [(b, g) for b in range(B) for g in range(C // K)]

        def load_x(i):
            b, g = units[i]
            return load("x%d" % i, x1_0[b, K * g : K * (g + 1), :], BF16)

        gates = {}
        x_raw = {}
        ug0 = (load("u0", u[0], BF16), load("g0", grad_out[0], BF16), load("c00", cand[0], F32, 0))
        w_first = [load("w20a", W_c[2 * C : 2 * C + K, :], BF16, 0)]
        gates[0] = ug0 + (load("c01", cand[0], F32, 1),)
        w_first.append(load("w20b", W_c[2 * C : 2 * C + K, :], BF16, 1))
        w_raw[2, 1] = load_w(2, 1)
        sup_raw = load("sup", support0, BF16)
        w_raw[1, 0] = load_w(1, 0)
        gates[1] = load_gates(1)
        w_raw[1, 1] = load_w(1, 1)
        for i in range(4):
            x_raw[i] = load_x(i)

        ident0 = keep.tile([P, P], F32, name="ident0")
        make_identity(nc, ident0[:])
        ident = keep.tile([P, P], F32, name="ident")
        nc.scalar.activation(out=ident[:], in_=ident0[:], func=ACT.Square)

        free_banks = list(range(8))
        bank_of = {}

        def take_bank():
            n = free_banks[0]
            free_banks.remove(n)
            bank = psum.tile([P, 512], F32, name="bank%d" % n, tag="bank%d" % n)
            bank_of[n] = bank
            return bank

        def give_bank(bank):
            free_banks.extend([n for n in range(8) if bank_of.get(n) is bank])

        def copy_on(eng, out, in_):
            if eng == "s":
                nc.scalar.copy(out=out, in_=in_)
            else:
                nc.vector.tensor_copy(out=out, in_=in_)

        def quantize(name, grouped, fmt):
            codes = keep.tile([P, 512], U32, name=name + "_codes", align_bytes=64)
            scales = keep.tile([P, 512], U8, name=name + "_scales", align_bytes=64)
            nc.vector.quantize_mx(out=codes[:].bitcast(fmt), scales=scales[:], in_=grouped[:])
            return (codes, scales, fmt)

        def mx(acc, stat, s, mov, start, stop):
            cols = slice(P * s, P * (s + 1))
            nc.tensor.matmul_mx(
                out=acc[:],
                lhsT=stat[0][:, cols].bitcast(stat[2]),
                lhsT_scale=stat[1][:, cols],
                rhs=mov[0][:].bitcast(mov[2]),
                rhs_scale=mov[1][:],
                start=start,
                stop=stop,
            )

        def interleave(eng, raw):
            grouped = work.tile([P, WIDE], BF16, name="grouped", tag="grouped", bufs=3, align_bytes=64)
            copy_on(
                eng,
                grouped[:].rearrange("p (c i t) -> p c t i", i=4, t=PACK),
                raw[:].rearrange("p (t c i) -> p c t i", i=4, t=PACK),
            )
            return grouped

        def interleave_dz1(eng, raw):
            grouped = work.tile([P, WIDE], BF16, name="grouped", tag="grouped", bufs=3, align_bytes=64)
            copy_on(
                eng,
                grouped[:].rearrange("p (w h e t) -> p h w t e", h=2, e=2, t=PACK),
                raw[:].rearrange("p (t h w e) -> p h w t e", h=2, e=2, t=PACK),
            )
            return grouped

        def keep_warm(bank, passes):
            for k in range(passes):
                mx(bank, wq[2, 0], 0, dz2q[0], True, True)

        def transposes(src, stepped, warm=0):
            words = src[:].bitcast(F32)
            banks = []
            for pair in range(2):
                bank = take_bank()
                if pair == 0:
                    keep_warm(bank, warm)
                for t2 in range(2):
                    for h in range(2):
                        w0 = 256 * (2 * pair + t2)
                        if stepped:
                            in_ = words[:, w0 + h : w0 + 256 : 2]
                        else:
                            in_ = words[:, w0 + P * h : w0 + P * (h + 1)]
                        slot = 2 * t2 + h
                        nc.tensor.transpose(bank[:, P * slot : P * (slot + 1)], in_, ident[:])
                banks.append(bank)
            return banks

        def transpose_half(src):
            words = src[:].bitcast(F32)
            bank = take_bank()
            for t2 in range(2):
                for h in range(2):
                    slot = 2 * t2 + h
                    nc.tensor.transpose(
                        bank[:, P * slot : P * (slot + 1)], words[:, 256 * t2 + h : 256 * (t2 + 1) : 2], ident[:]
                    )
            return bank

        def new_turned():
            turned = work.tile([P, WIDE], BF16, name="turned", tag="turned", bufs=3, align_bytes=64)
            return turned

        def empty_bank(eng, turned, banks, pair):
            words = turned[:].bitcast(F32)
            copy_on(
                eng,
                words[:, 512 * pair : 512 * (pair + 1)].rearrange("p (t c h) -> p t c h", t=2, h=2),
                banks[pair][:].rearrange("p (t h c) -> p t c h", t=2, h=2),
            )
            give_bank(banks[pair])

        def empty_transposes(engs, banks):
            turned = new_turned()
            for pair in range(2):
                empty_bank(engs[pair], turned, banks, pair)
            return turned

        def gate_product(b, h):
            a = work.tile([P, 1024], F32, name="a", tag="a")
            nc.vector.scalar_tensor_tensor(
                out=a[:], in0=gates[b][0][:, 1024 * h : 1024 * (h + 1)], scalar=1.0, in1=gates[b][1][:, 1024 * h : 1024 * (h + 1)], op0=ALU.subtract, op1=ALU.mult
            )
            return a

        def square(b, h):
            s = work.tile([P, 1024], F32, name="s", tag="s")
            nc.scalar.activation(
                out=s[:].rearrange("p (n e) -> p n e", e=2),
                in_=gates[b][2 + h][:].rearrange("p (e n) -> p n e", e=2),
                func=ACT.Square,
            )
            return s

        def dz2_half(dz2, h, s, a):
            nc.vector.scalar_tensor_tensor(
                out=dz2[:, 1024 * h : 1024 * (h + 1)].rearrange("p (n e) -> p n e", e=2),
                in0=s[:].rearrange("p (n e) -> p n e", e=2),
                scalar=1.0,
                in1=a[:].rearrange("p (e n) -> p n e", e=2),
                op0=ALU.subtract,
                op1=ALU.mult,
            )

        def interleave_pairs(dz2):
            grouped = work.tile([P, WIDE], BF16, name="grouped", tag="grouped", bufs=3, align_bytes=64)
            nc.vector.tensor_copy(
                out=grouped[:].bitcast(F32).rearrange("p (n h) -> p n h", h=2),
                in_=dz2[:].bitcast(F32).rearrange("p (h n) -> p n h", h=2),
            )
            return grouped

        def square_cols(s, b, h, n0):
            nc.scalar.activation(
                out=s[:].rearrange("p (n e) -> p n e", e=2)[:, n0 : n0 + 256, :],
                in_=gates[b][2 + h][:].rearrange("p (e n) -> p n e", e=2)[:, n0 : n0 + 256, :],
                func=ACT.Square,
            )

        def dz2_cols(dz2, h, s, a, n0):
            nc.vector.scalar_tensor_tensor(
                out=dz2[:, 1024 * h : 1024 * (h + 1)].rearrange("p (n e) -> p n e", e=2)[:, n0 : n0 + 256, :],
                in0=s[:].rearrange("p (n e) -> p n e", e=2)[:, n0 : n0 + 256, :],
                scalar=1.0,
                in1=a[:].rearrange("p (e n) -> p n e", e=2)[:, n0 : n0 + 256, :],
                op0=ALU.subtract,
                op1=ALU.mult,
            )

        def pairs_cols(grouped, dz2, n0):
            nc.vector.tensor_copy(
                out=grouped[:].bitcast(F32).rearrange("p (n h) -> p n h", h=2)[:, n0 : n0 + 256, :],
                in_=dz2[:].bitcast(F32).rearrange("p (h n) -> p n h", h=2)[:, n0 : n0 + 256, :],
            )

        wq = {}
        dz2q = {}
        dz1 = {}
        dz1_nodes = {}
        dz1_chan = {}
        xq = {}

        def dh_x2(i, slots=range(PACK), warm=0):
            b, g = units[i]
            banks = []
            for t in slots:
                banks.append(take_bank())
                keep_warm(banks[-1], warm)
            for k, t in enumerate(slots):
                mx(banks[k], wq[2, g], t, dz2q[b], True, True)
            return banks

        def round_dz1(i, banks, engs, slots=range(PACK)):
            if i not in dz1:
                dz1[i] = keep.tile([P, WIDE], BF16, name="dz1_%d" % i, align_bytes=64)
            for k, t in enumerate(slots):
                out = dz1[i][:, 512 * t : 512 * (t + 1)].rearrange("p (h w e) -> p h w e", h=2, e=2)
                in_ = banks[k][:].rearrange("p (w h e) -> p h w e", h=2, e=2)
                if engs[k] == "s":
                    nc.scalar.activation(out=out, in_=in_, func=ACT.Copy, scale=2.0)
                else:
                    nc.vector.tensor_scalar(out=out, in0=in_, scalar1=2.0, scalar2=None, op0=ALU.mult)
                give_bank(banks[k])

        def dx_open(i, pair):
            b, g = units[i]
            banks = []
            for t in (2 * pair, 2 * pair + 1):
                bank = take_bank()
                mx(bank, wq[1, g], t, dz2q[b], True, False)
                banks.append(bank)
            return banks

        def dx_close(i, pair, banks):
            for k in range(2):
                mx(banks[k], dz1_nodes[i], 2 * pair + k, supq, False, True)

        def dx_pair(i, pair, warm=0):
            b, g = units[i]
            banks = []
            for t in (2 * pair, 2 * pair + 1):
                bank = take_bank()
                if t == 2 * pair:
                    keep_warm(bank, warm)
                mx(bank, wq[1, g], t, dz2q[b], True, False)
                mx(bank, dz1_nodes[i], t, supq, False, True)
                banks.append(bank)
            return banks

        def store_pair(banks, engs, dst, split=False):
            res = work.tile([P, 1024], F32, name="res", tag="res", bufs=6)
            for k in range(2):
                copy_on(engs[k], res[:, 512 * k : 512 * (k + 1)], banks[k][:])
                give_bank(banks[k])
                if split:
                    nc.sync.dma_start(out=dst[:, k, :], in_=res[:, 512 * k : 512 * (k + 1)])
            if not split:
                nc.sync.dma_start(out=dst, in_=res[:].rearrange("p (k m) -> p k m", k=2))

        def store_one(bank, eng, dst):
            res1 = work.tile([P, 512], F32, name="res1", tag="res1", bufs=8)
            copy_on(eng, res1[:], bank[:])
            give_bank(bank)
            nc.sync.dma_start(out=dst, in_=res1[:])

        def interleave_half(raw, grouped, h):
            nc.vector.tensor_copy(
                out=grouped[:, 1024 * h : 1024 * (h + 1)].rearrange("p (c i t) -> p c t i", i=4, t=PACK),
                in_=raw[:].rearrange("p (t h c i) -> p h c t i", i=4, t=PACK, h=2)[:, h],
            )

        def quantize_half(q, grouped, h):
            nc.vector.quantize_mx(
                out=q[0][:, 256 * h : 256 * (h + 1)].bitcast(q[2]),
                scales=q[1][:, 256 * h : 256 * (h + 1)],
                in_=grouped[:, 1024 * h : 1024 * (h + 1)],
            )

        def new_codes(name, fmt):
            codes = keep.tile([P, 512], U32, name=name + "_codes", align_bytes=64)
            scales = keep.tile([P, 512], U8, name=name + "_scales", align_bytes=64)
            return (codes, scales, fmt)

        def out0_view(i, pair):
            b, g = units[i]
            rows = out_0[b, K * g : K * (g + 1), :].rearrange("(p t) m -> p t m", t=PACK)
            return rows[:, 2 * pair : 2 * pair + 2, :]

        warm_mov = quantize("warm_mov", gates[0][0], E4M3)
        warm_stat = new_codes("warm_stat", E5M2)
        nc.vector.quantize_mx(out=warm_stat[0][:, 0:P].bitcast(E5M2), scales=warm_stat[1][:, 0:P], in_=gates[0][0][:, 0:512])
        warm_bank = take_bank()

        def warm_up(passes):
            for k in range(passes):
                mx(warm_bank, warm_stat, 0, warm_mov, True, True)

        warm_up(4)
        a0 = gate_product(0, 0)
        a1 = gate_product(0, 1)
        s0 = square(0, 0)
        dz2 = work.tile([P, WIDE], BF16, name="dz2", tag="dz2")
        dz2_half(dz2, 0, s0, a0)
        tw = [transpose_half(w_first[0])]
        warm_up(3)
        tw.append(transpose_half(w_first[1]))
        warm_up(2)
        s1 = work.tile([P, 1024], F32, name="s", tag="s")
        turned = new_turned()
        square_cols(s1, 0, 1, 0)
        square_cols(s1, 0, 1, 256)
        empty_bank("s", turned, tw, 0)
        empty_bank("s", turned, tw, 1)
        dz2_cols(dz2, 1, s1, a1, 0)
        dz2_cols(dz2, 1, s1, a1, 256)
        grouped = work.tile([P, WIDE], BF16, name="grouped", tag="grouped", bufs=3, align_bytes=64)
        wq[2, 0] = new_codes("w20", E4M3)
        dz2q[0] = new_codes("dz20", E5M2)
        pairs_cols(grouped, dz2, 0)
        quantize_half(wq[2, 0], turned, 0)
        pairs_cols(grouped, dz2, 256)
        quantize_half(dz2q[0], grouped, 0)
        quantize_half(dz2q[0], grouped, 1)
        quantize_half(wq[2, 0], turned, 1)
        tw = transposes(w_raw[2, 1], True)
        warm_up(2)
        give_bank(warm_bank)
        m0 = dh_x2(0)
        turned = empty_transposes("ss", tw)
        sup_g = interleave("v", sup_raw)
        wq[2, 1] = quantize("w21", turned, E4M3)
        supq = quantize("sup", sup_g, E4M3)
        a0 = gate_product(1, 0)
        tw = transposes(w_raw[1, 0], True)
        round_dz1(0, m0, "ssss")
        ta = transposes(dz1[0], False, 2)
        m1 = dh_x2(1)
        a1 = gate_product(1, 1)
        turned = empty_transposes("ss", tw)
        tw = transposes(w_raw[1, 1], True, 3)
        gb = interleave_dz1("v", dz1[0])
        turned_a = empty_transposes("ss", ta)
        wq[1, 0] = quantize("w10", turned, E4M3)
        dz1_nodes[0] = quantize("a0", turned_a, E5M2)
        oa = dx_pair(0, 0, 0)
        s0 = square(1, 0)
        s1 = square(1, 1)
        dz2 = work.tile([P, WIDE], BF16, name="dz2", tag="dz2")
        dz2_half(dz2, 0, s0, a0)
        dz2_half(dz2, 1, s1, a1)
        round_dz1(1, m1, "ssss")
        ob = dx_pair(0, 1)
        ta = transposes(dz1[1], False)
        dz1_chan[0] = quantize("b0", gb, E5M2)
        grouped = interleave_pairs(dz2)
        gx = interleave("v", x_raw[0])
        dz2q[1] = quantize("dz21", grouped, E5M2)
        xq[0] = quantize("x0", gx, E4M3)
        turned = empty_transposes("ss", tw)
        turned_a = empty_transposes("ss", ta)
        m2 = dh_x2(2, warm=1)
        gb = interleave_dz1("v", dz1[1])
        gx = interleave("v", x_raw[1])
        dz1_chan[1] = quantize("b1", gb, E5M2)
        xq[1] = quantize("x1", gx, E4M3)
        wq[1, 1] = quantize("w11", turned, E4M3)
        dz1_nodes[1] = quantize("a1", turned_a, E5M2)
        store_pair(oa, "ss", out0_view(0, 0))
        store_pair(ob, "ss", out0_view(0, 1))
        ds = [take_bank(), take_bank(), take_bank(), take_bank()]

        def ds_pass(i, slices=(0, 1, 2, 3)):
            for s in slices:
                mx(ds[s], dz1_chan[i], s, xq[i], i == 0, i == 3)

        ds_pass(0, (0, 1, 2, 3))
        round_dz1(2, m2, "ssss")
        m3 = dh_x2(3, (0, 1))
        ta = transposes(dz1[2], False, 1)
        gx = interleave("v", x_raw[2])
        round_dz1(3, m3, "ss", (0, 1))
        m3 = dh_x2(3, (2, 3))
        ds_pass(1)
        turned_a = empty_transposes("ss", ta)
        gb = interleave_dz1("v", dz1[2])
        round_dz1(3, m3, "ss", (2, 3))
        oa = dx_pair(1, 0)
        ta = transposes(dz1[3], False)
        dz1_nodes[2] = quantize("a2", turned_a, E5M2)
        xq[2] = quantize("x2", gx, E4M3)
        dz1_chan[2] = quantize("b2", gb, E5M2)
        store_pair(oa, "ss", out0_view(1, 0))
        ob = dx_pair(1, 1)
        turned_a = empty_transposes("ss", ta)
        oa = dx_pair(2, 0)
        gx = interleave("v", x_raw[3])
        dz1_nodes[3] = quantize("a3", turned_a, E5M2)
        gb = interleave_dz1("v", dz1[3])
        xq[3] = quantize("x3", gx, E4M3)
        dz1_chan[3] = quantize("b3", gb, E5M2)
        store_pair(ob, "ss", out0_view(1, 1))
        ob = dx_pair(2, 1)
        store_pair(oa, "ss", out0_view(2, 0))
        oa = dx_pair(3, 0)
        store_pair(ob, "ss", out0_view(2, 1))
        ob = dx_pair(3, 1)
        for s in (0, 1, 2, 3):
            ds_pass(2, (s,))
            ds_pass(3, (s,))
        rows1 = out_1.rearrange("(h k p) m -> h p k m", h=2, k=2)
        store_pair(oa, "ss", out0_view(3, 0))
        store_pair(ob, "vs", out0_view(3, 1))
        store_pair([ds[0], ds[1]], "vs", rows1[0])
        store_pair([ds[2], ds[3]], "vs", rows1[1], split=True)
